import numpy as np
import ml_dtypes


def mxq(x, axis, fmt="e4m3"):
    dtype, down = {"e4m3": (ml_dtypes.float8_e4m3fn, 7), "e5m2": (ml_dtypes.float8_e5m2, 14)}[fmt]
    v = np.moveaxis(np.asarray(x, np.float32).astype(ml_dtypes.bfloat16).astype(np.float64), axis, -1)
    blocks = v.reshape(v.shape[:-1] + (-1, 32))
    amax = np.abs(blocks).max(-1, keepdims=True)
    byte = np.maximum(np.where(amax > 0, np.frexp(amax)[1] - 1 + 127, 0) - down, 1)
    scale = np.exp2(byte - 127.0)
    codes = (blocks / scale).astype(np.float32).astype(dtype).astype(np.float64)
    return np.moveaxis((codes * scale).reshape(v.shape), -1, axis)


WIDE = False


def mx_kscale(k):
    if not WIDE:
        return np.ones(k)
    levels = np.array([10, -10, 5, -5, 0])
    a = np.random.permutation(np.resize(levels, k // 512 * 4)).reshape(k // 512, 4)
    idx = np.arange(k)
    return np.exp2(a[idx // 512, idx % 128 // 32])


BF16 = ml_dtypes.bfloat16


def bf(x):
    return np.asarray(x, np.float32).astype(BF16)


def f64(x):
    return np.asarray(x).astype(np.float64)


E2M1 = np.array([0.0, 0.5, 1.0, 1.5, 2.0, 3.0, 4.0, 6.0, -0.0, -0.5, -1.0, -1.5, -2.0, -3.0, -4.0, -6.0])


def pack_weight(w, fmt):
    k, n = w.shape
    w = f64(bf(w)).reshape(k // 32, 32, n)
    amax = np.abs(w).max(1)
    if fmt == "e4m3":
        byte = np.frexp(amax)[1] - 1 + 127 - 7
    else:
        mant, ex = np.frexp(amax / 6.0)
        byte = np.where(mant > 0.5, ex, ex - 1) + 127
    byte = np.clip(np.where(amax > 0, byte, 1), 1, 254)
    scaled = (w * np.exp2(127.0 - byte)[:, None, :]).reshape(k, n).astype(np.float32)
    by_word = np.ascontiguousarray(scaled.reshape(k // 512, 128, 4, n).transpose(0, 1, 3, 2))
    if fmt == "e4m3":
        words = by_word.astype(ml_dtypes.float8_e4m3fn).view(np.uint8)
    else:
        c = by_word.astype(ml_dtypes.float4_e2m1fn).view(np.uint8) & 0xF
        words = c[..., 0::2] | (c[..., 1::2] << 4)
    return np.ascontiguousarray(words), np.ascontiguousarray(byte.astype(np.uint8).reshape(k // 512, 16, n))


def unpack_weight(words, scales, fmt):
    g, p, n, _ = words.shape
    if fmt == "e4m3":
        vals = np.ascontiguousarray(words).view(ml_dtypes.float8_e4m3fn).astype(np.float64)
    else:
        nib = np.empty((g, p, n, 4), np.uint8)
        nib[..., 0::2] = words & 0xF
        nib[..., 1::2] = words >> 4
        vals = E2M1[nib]
    vals = vals * np.repeat(np.exp2(scales.astype(np.float64) - 127.0), 8, axis=1)[..., None]
    return vals.transpose(0, 1, 3, 2).reshape(g * 512, n)


E, CAP, D_IN, D_OUT, B, L = 8, 256, 2048, 512, 4, 256
S = B * L


def setup_inputs():
    s = mx_kscale(D_IN)
    inputs = bf(np.random.standard_normal((E * CAP, D_IN)) * s)
    combine_weights = bf(np.random.uniform(0.0, 1.0, (S, E, CAP)) * 2.0 / np.sqrt(E * CAP))
    stack = np.random.standard_normal((E, D_IN, D_OUT)) / np.sqrt(D_IN) / s[None, :, None]
    weight_words, weight_scales = pack_weight(stack.reshape(-1, D_OUT), "e4m3")
    bias = bf(np.random.standard_normal((E, 1, D_OUT)) * 0.1)
    return {"inputs": inputs,
            "combine_weights": combine_weights,
            "weight_words": weight_words,
            "weight_scales": weight_scales,
            "bias": bias}


def reference(inputs, combine_weights, weight_words, weight_scales, bias):
    x = f64(inputs).reshape(E, CAP, D_IN)
    w = unpack_weight(weight_words, weight_scales, "e4m3").reshape(E, D_IN, D_OUT)
    expert_out = (mxq(x, 2, "e4m3") @ w) + f64(bias)
    expert_out = expert_out.reshape(E, 1, CAP, D_OUT).transpose(1, 0, 2, 3)
    flat = expert_out.reshape(E * CAP, D_OUT)
    cw = f64(combine_weights).reshape(S, E * CAP)
    output = mxq(cw, 1, "e4m3") @ mxq(flat, 0, "e4m3")
    return output.reshape(B, L, D_OUT)

@@ -1,0 +1,214 @@
+from contextlib import ExitStack
+
+import concourse.mybir as mybir
+from concourse.masks import make_identity
+
+F32 = mybir.dt.float32
+BF16 = mybir.dt.bfloat16
+I32 = mybir.dt.int32
+U32 = mybir.dt.uint32
+U8 = mybir.dt.uint8
+FP8X4 = mybir.dt.float8_e4m3fn_x4
+
+P = 128
+PACK = 4
+K_PASS = P * PACK
+K_WORDS = K_PASS // 2
+
+EXPERTS = 8
+CAP = 256
+D_IN = 2048
+D_OUT = 512
+TOKENS = 1024
+ROW_LEN = 2048
+PASSES = ROW_LEN // K_PASS
+ROWS = 2
+TOKEN_TILES = TOKENS // P
+CW_BLOCKS = TOKEN_TILES // ROWS
+BLOCKS = EXPERTS + CW_BLOCKS
+N_HALF = D_OUT // 2
+AHEAD = 3
+
+FLOPS = 2 * EXPERTS * CAP * D_IN * D_OUT + 2 * TOKENS * EXPERTS * CAP * D_OUT
+
+
+def every_second_word(g, u):
+    return slice(K_WORDS * g + u, K_WORDS * (g + 1), 2)
+
+
+def half_of_the_words(g, u):
+    return slice(K_WORDS * g + P * u, K_WORDS * g + P * (u + 1))
+
+
+def tile_expertparallelbehindblock_e_kernel(
+    tc, inputs, combine_weights, weight_words, weight_scales, bias, out
+):
+    nc = tc.nc
+
+    x_view = inputs.rearrange("(e p a) k -> e p a k", p=P, a=ROWS)
+    cw_view = combine_weights.rearrange("(p t) e c -> p t (e c)", t=TOKEN_TILES)
+    out_view = out.rearrange("b l n -> (b l) n").rearrange("(p t) n -> p t n", t=TOKEN_TILES)
+    words_view = weight_words.rearrange("(e g) p n t -> e p g (n t)", g=PASSES)
+    scales_view = weight_scales.rearrange("(e g) (q r) n -> e q g r n", g=PASSES, r=4)
+
+    with ExitStack() as ctx:
+        const = ctx.enter_context(tc.tile_pool(name="const", bufs=1))
+        raw_pool = ctx.enter_context(tc.tile_pool(name="raw", bufs=AHEAD + 1))
+        words_pool = ctx.enter_context(tc.tile_pool(name="words", bufs=AHEAD + 1))
+        grouped_pool = ctx.enter_context(tc.tile_pool(name="grouped", bufs=2))
+        codes_pool = ctx.enter_context(tc.tile_pool(name="codes", bufs=2))
+        flat_pool = ctx.enter_context(tc.tile_pool(name="flat", bufs=2))
+        out_pool = ctx.enter_context(tc.tile_pool(name="result", bufs=2))
+        turned_psum = ctx.enter_context(tc.psum_pool(name="turned", bufs=4))
+        sums_psum = ctx.enter_context(tc.psum_pool(name="sums", bufs=4))
+        ctx.enter_context(tc.manual_schedule())
+
+        raw_tiles = {}
+        word_tiles = {}
+        quantised = {}
+        flat_tiles = {}
+
+        w_planes = const.tile([P, EXPERTS, D_OUT], U8, align_bytes=64)
+        nc.vector.memset(w_planes[:].rearrange("p e n -> p (e n)").bitcast(I32), 0)
+        flat_codes = const.tile([P, PASSES, D_OUT], U32, align_bytes=64)
+        flat_planes = const.tile([P, PASSES, D_OUT], U8, align_bytes=64)
+
+        def load_raw(b):
+            raw = raw_pool.tile([P, ROWS, ROW_LEN], BF16)
+            if b < EXPERTS:
+                nc.sync.dma_start(out=raw[:], in_=x_view[b])
+            else:
+                first = ROWS * (b - EXPERTS)
+                nc.sync.dma_start(out=raw[:], in_=cw_view[:, first : first + ROWS, :])
+            raw_tiles[b] = raw
+
+        def load_for_block(b):
+            if b < EXPERTS:
+                for q in range(4):
+                    nc.sync.dma_start(
+                        out=w_planes[32 * q : 32 * q + 16, b, :].bitcast(I32),
+                        in_=scales_view[b, q].bitcast(I32),
+                    )
+            if b + 1 < BLOCKS:
+                load_raw(b + 1)
+            if b < EXPERTS:
+                w_words = words_pool.tile([P, PASSES, D_OUT], U32, align_bytes=64)
+                nc.sync.dma_start(out=w_words[:].bitcast(I32), in_=words_view[b].bitcast(I32))
+                word_tiles[b] = w_words
+
+        load_raw(0)
+        for b in range(AHEAD):
+            load_for_block(b)
+
+        ident_bf = const.tile([P, P], BF16)
+        make_identity(nc, ident_bf[:])
+        ident_f32 = const.tile([P, P], F32)
+        make_identity(nc, ident_f32[:])
+        bias_rows = const.tile([P, D_OUT], BF16)
+        nc.vector.memset(bias_rows[:], 0.0)
+        nc.scalar.dma_start(out=bias_rows[0:EXPERTS, :], in_=bias.rearrange("e o n -> (e o) n"))
+        bias_all = const.tile([P, EXPERTS, D_OUT], BF16)
+        for e in range(EXPERTS):
+            spread = sums_psum.tile([P, D_OUT], F32, tag="sums")
+            nc.tensor.matmul(
+                out=spread[:],
+                lhsT=ident_bf[:, e : e + 1].to_broadcast([P, P]),
+                rhs=bias_rows[:],
+                start=True,
+                stop=True,
+            )
+            if e % 2 == 0:
+                nc.vector.tensor_copy(out=bias_all[:, e, :], in_=spread[:])
+            else:
+                nc.scalar.copy(out=bias_all[:, e, :], in_=spread[:])
+
+        def prepare(b):
+            raw = raw_tiles[b]
+            word_columns = every_second_word if b < EXPERTS else half_of_the_words
+            grouped = grouped_pool.tile([P, PASSES, ROWS, P, PACK], BF16, align_bytes=64)
+            for a in range(ROWS):
+                raw_words = raw[:, a, :].bitcast(F32)
+                for first_pass in range(0, PASSES, 2):
+                    turned = turned_psum.tile([P, 2, 2, P], F32, tag="turned")
+                    for i in range(2):
+                        for u in range(2):
+                            nc.tensor.transpose(
+                                turned[:, i, u, :],
+                                raw_words[:, word_columns(first_pass + i, u)],
+                                ident_f32[:],
+                            )
+                    nc.scalar.copy(
+                        out=grouped[:, first_pass : first_pass + 2, a].bitcast(F32),
+                        in_=turned[:].rearrange("p i u r -> p i r u"),
+                    )
+            codes = codes_pool.tile([P, PASSES, ROWS, P], U32, align_bytes=64)
+            planes = codes_pool.tile([P, PASSES, ROWS, P], U8, align_bytes=64)
+            nc.vector.quantize_mx(
+                out=codes[:].rearrange("p g a r -> p (g a r)").bitcast(FP8X4),
+                scales=planes[:].rearrange("p g a r -> p (g a r)"),
+                in_=grouped[:].rearrange("p g a r t -> p (g a r t)"),
+            )
+            quantised[b] = (codes, planes)
+
+        def expert_matmuls(e):
+            codes, planes = quantised[e]
+            w_words = word_tiles[e]
+            g2, u = divmod(e, 2)
+            if u == 0:
+                flat_grouped = flat_pool.tile([P, D_OUT, 2, ROWS], BF16, align_bytes=64)
+                flat_tiles[g2] = flat_grouped
+            flat_grouped = flat_tiles[g2]
+            for first_col in range(0, D_OUT, N_HALF):
+                cols = slice(first_col, first_col + N_HALF)
+                sums = sums_psum.tile([P, ROWS, N_HALF], F32, tag="sums")
+                for a in range(ROWS):
+                    for g in range(PASSES):
+                        nc.tensor.matmul_mx(
+                            out=sums[:, a, :],
+                            lhsT=codes[:, g, a, :].bitcast(FP8X4),
+                            lhsT_scale=planes[:, g, a, :],
+                            rhs=w_words[:, g, cols].bitcast(FP8X4),
+                            rhs_scale=w_planes[4 * g : P, e, cols],
+                            start=(g == 0),
+                            stop=(g == PASSES - 1),
+                        )
+                nc.vector.tensor_tensor(
+                    out=flat_grouped[:, cols, u, :],
+                    in0=sums[:].rearrange("p a n -> p n a"),
+                    in1=bias_all[:, e, cols].unsqueeze(2).to_broadcast([P, N_HALF, ROWS]),
+                    op=mybir.AluOpType.add,
+                )
+            if u == 1:
+                nc.vector.quantize_mx(
+                    out=flat_codes[:, g2, :].bitcast(FP8X4),
+                    scales=flat_planes[:, g2, :],
+                    in_=flat_grouped[:].rearrange("p n u a -> p (n u a)"),
+                )
+
+        def combine_matmuls(c):
+            codes, planes = quantised[EXPERTS + c]
+            result = out_pool.tile([P, ROWS, D_OUT], F32)
+            for a in range(ROWS):
+                sums = sums_psum.tile([P, D_OUT], F32, tag="sums")
+                for g in range(PASSES):
+                    nc.tensor.matmul_mx(
+                        out=sums[:],
+                        lhsT=codes[:, g, a, :].bitcast(FP8X4),
+                        lhsT_scale=planes[:, g, a, :],
+                        rhs=flat_codes[:, g, :].bitcast(FP8X4),
+                        rhs_scale=flat_planes[:, g, :],
+                        start=(g == 0),
+                        stop=(g == PASSES - 1),
+                    )
+                nc.vector.tensor_copy(out=result[:, a, :], in_=sums[:])
+            nc.sync.dma_start(out=out_view[:, ROWS * c : ROWS * (c + 1), :], in_=result[:])
+
+        prepare(0)
+        for b in range(BLOCKS):
+            load_for_block(b + AHEAD)
+            if b + 1 < BLOCKS:
+                prepare(b + 1)
+            if b < EXPERTS:
+                expert_matmuls(b)
+            else:
+                combine_matmuls(b - EXPERTS)

@@ -96,6 +96,12 @@ def tile_expertparallelbehindblock_e_kernel(
                 nc.sync.dma_start(out=w_words[:].bitcast(I32), in_=words_view[b].bitcast(I32))
                 word_tiles[b] = w_words
 
+        bias_rows = const.tile([P, D_OUT], BF16)
+        nc.sync.dma_start(
+            out=bias_rows[:],
+            in_=bias.rearrange("e o n -> o e n").to_broadcast([P // EXPERTS, EXPERTS, D_OUT]),
+        )
+
         load_raw(0)
         for b in range(AHEAD):
             load_for_block(b)
@@ -104,9 +110,6 @@ def tile_expertparallelbehindblock_e_kernel(
         make_identity(nc, ident_bf[:])
         ident_f32 = const.tile([P, P], F32)
         make_identity(nc, ident_f32[:])
-        bias_rows = const.tile([P, D_OUT], BF16)
-        nc.vector.memset(bias_rows[:], 0.0)
-        nc.scalar.dma_start(out=bias_rows[0:EXPERTS, :], in_=bias.rearrange("e o n -> (e o) n"))
         bias_all = const.tile([P, EXPERTS, D_OUT], BF16)
         for e in range(EXPERTS):
             spread = sums_psum.tile([P, D_OUT], F32, tag="sums")

@@ -27,7 +27,6 @@ TOKEN_TILES = TOKENS // P
 CW_BLOCKS = TOKEN_TILES // ROWS
 BLOCKS = EXPERTS + CW_BLOCKS
 N_HALF = D_OUT // 2
-AHEAD = 3
 
 FLOPS = 2 * EXPERTS * CAP * D_IN * D_OUT + 2 * TOKENS * EXPERTS * CAP * D_OUT
 
@@ -53,8 +52,8 @@ def tile_expertparallelbehindblock_e_kernel(
 
     with ExitStack() as ctx:
         const = ctx.enter_context(tc.tile_pool(name="const", bufs=1))
-        raw_pool = ctx.enter_context(tc.tile_pool(name="raw", bufs=AHEAD + 1))
-        words_pool = ctx.enter_context(tc.tile_pool(name="words", bufs=AHEAD + 1))
+        raw_pool = ctx.enter_context(tc.tile_pool(name="raw", bufs=BLOCKS))
+        words_pool = ctx.enter_context(tc.tile_pool(name="words", bufs=EXPERTS))
         grouped_pool = ctx.enter_context(tc.tile_pool(name="grouped", bufs=2))
         codes_pool = ctx.enter_context(tc.tile_pool(name="codes", bufs=2))
         flat_pool = ctx.enter_context(tc.tile_pool(name="flat", bufs=2))
@@ -103,7 +102,7 @@ def tile_expertparallelbehindblock_e_kernel(
         )
 
         load_raw(0)
-        for b in range(AHEAD):
+        for b in range(BLOCKS):
             load_for_block(b)
 
         ident_bf = const.tile([P, P], BF16)
@@ -208,7 +207,6 @@ def tile_expertparallelbehindblock_e_kernel(
 
         prepare(0)
         for b in range(BLOCKS):
-            load_for_block(b + AHEAD)
             if b + 1 < BLOCKS:
                 prepare(b + 1)
             if b < EXPERTS:

@@ -54,8 +54,8 @@ def tile_expertparallelbehindblock_e_kernel(
         const = ctx.enter_context(tc.tile_pool(name="const", bufs=1))
         raw_pool = ctx.enter_context(tc.tile_pool(name="raw", bufs=BLOCKS))
         words_pool = ctx.enter_context(tc.tile_pool(name="words", bufs=EXPERTS))
-        grouped_pool = ctx.enter_context(tc.tile_pool(name="grouped", bufs=2))
-        codes_pool = ctx.enter_context(tc.tile_pool(name="codes", bufs=2))
+        grouped_pool = ctx.enter_context(tc.tile_pool(name="grouped", bufs=4))
+        codes_pool = ctx.enter_context(tc.tile_pool(name="codes", bufs=4))
         flat_pool = ctx.enter_context(tc.tile_pool(name="flat", bufs=2))
         out_pool = ctx.enter_context(tc.tile_pool(name="result", bufs=2))
         turned_psum = ctx.enter_context(tc.psum_pool(name="turned", bufs=4))
@@ -66,6 +66,8 @@ def tile_expertparallelbehindblock_e_kernel(
         word_tiles = {}
         quantised = {}
         flat_tiles = {}
+        sums_tiles = {}
+        result_tiles = {}
 
         w_planes = const.tile([P, EXPERTS, D_OUT], U8, align_bytes=64)
         nc.vector.memset(w_planes[:].rearrange("p e n -> p (e n)").bitcast(I32), 0)
@@ -124,92 +126,107 @@ def tile_expertparallelbehindblock_e_kernel(
             else:
                 nc.scalar.copy(out=bias_all[:, e, :], in_=spread[:])
 
-        def prepare(b):
-            raw = raw_tiles[b]
+        def prepare(b, a):
+            raw_words = raw_tiles[b][:, a, :].bitcast(F32)
             word_columns = every_second_word if b < EXPERTS else half_of_the_words
-            grouped = grouped_pool.tile([P, PASSES, ROWS, P, PACK], BF16, align_bytes=64)
-            for a in range(ROWS):
-                raw_words = raw[:, a, :].bitcast(F32)
-                for first_pass in range(0, PASSES, 2):
-                    turned = turned_psum.tile([P, 2, 2, P], F32, tag="turned")
-                    for i in range(2):
-                        for u in range(2):
-                            nc.tensor.transpose(
-                                turned[:, i, u, :],
-                                raw_words[:, word_columns(first_pass + i, u)],
-                                ident_f32[:],
-                            )
-                    nc.scalar.copy(
-                        out=grouped[:, first_pass : first_pass + 2, a].bitcast(F32),
-                        in_=turned[:].rearrange("p i u r -> p i r u"),
-                    )
-            codes = codes_pool.tile([P, PASSES, ROWS, P], U32, align_bytes=64)
-            planes = codes_pool.tile([P, PASSES, ROWS, P], U8, align_bytes=64)
+            grouped = grouped_pool.tile([P, PASSES, P, PACK], BF16, align_bytes=64)
+            for first_pass in range(0, PASSES, 2):
+                turned = turned_psum.tile([P, 2, 2, P], F32, tag="turned")
+                for i in range(2):
+                    for u in range(2):
+                        nc.tensor.transpose(
+                            turned[:, i, u, :],
+                            raw_words[:, word_columns(first_pass + i, u)],
+                            ident_f32[:],
+                        )
+                nc.scalar.copy(
+                    out=grouped[:, first_pass : first_pass + 2].bitcast(F32),
+                    in_=turned[:].rearrange("p i u r -> p i r u"),
+                )
+            codes = codes_pool.tile([P, PASSES, P], U32, align_bytes=64)
+            planes = codes_pool.tile([P, PASSES, P], U8, align_bytes=64)
             nc.vector.quantize_mx(
-                out=codes[:].rearrange("p g a r -> p (g a r)").bitcast(FP8X4),
-                scales=planes[:].rearrange("p g a r -> p (g a r)"),
-                in_=grouped[:].rearrange("p g a r t -> p (g a r t)"),
+                out=codes[:].rearrange("p g r -> p (g r)").bitcast(FP8X4),
+                scales=planes[:].rearrange("p g r -> p (g r)"),
+                in_=grouped[:].rearrange("p g r t -> p (g r t)"),
             )
-            quantised[b] = (codes, planes)
+            quantised[b, a] = (codes, planes)
 
-        def expert_matmuls(e):
-            codes, planes = quantised[e]
+        def expert_matmuls(e, a):
+            codes, planes = quantised[e, a]
             w_words = word_tiles[e]
             g2, u = divmod(e, 2)
-            if u == 0:
+            if u == 0 and a == 0:
                 flat_grouped = flat_pool.tile([P, D_OUT, 2, ROWS], BF16, align_bytes=64)
                 flat_tiles[g2] = flat_grouped
             flat_grouped = flat_tiles[g2]
-            for first_col in range(0, D_OUT, N_HALF):
-                cols = slice(first_col, first_col + N_HALF)
-                sums = sums_psum.tile([P, ROWS, N_HALF], F32, tag="sums")
-                for a in range(ROWS):
-                    for g in range(PASSES):
-                        nc.tensor.matmul_mx(
-                            out=sums[:, a, :],
-                            lhsT=codes[:, g, a, :].bitcast(FP8X4),
-                            lhsT_scale=planes[:, g, a, :],
-                            rhs=w_words[:, g, cols].bitcast(FP8X4),
-                            rhs_scale=w_planes[4 * g : P, e, cols],
-                            start=(g == 0),
-                            stop=(g == PASSES - 1),
-                        )
-                nc.vector.tensor_tensor(
-                    out=flat_grouped[:, cols, u, :],
-                    in0=sums[:].rearrange("p a n -> p n a"),
-                    in1=bias_all[:, e, cols].unsqueeze(2).to_broadcast([P, N_HALF, ROWS]),
-                    op=mybir.AluOpType.add,
-                )
-            if u == 1:
+            for half in range(D_OUT // N_HALF):
+                cols = slice(half * N_HALF, (half + 1) * N_HALF)
+                if a == 0:
+                    sums = sums_psum.tile([P, ROWS, N_HALF], F32, tag="sums")
+                    sums_tiles[e, half] = sums
+                sums = sums_tiles[e, half]
+                for g in range(PASSES):
+                    nc.tensor.matmul_mx(
+                        out=sums[:, a, :],
+                        lhsT=codes[:, g, :].bitcast(FP8X4),
+                        lhsT_scale=planes[:, g, :],
+                        rhs=w_words[:, g, cols].bitcast(FP8X4),
+                        rhs_scale=w_planes[4 * g : P, e, cols],
+                        start=(g == 0),
+                        stop=(g == PASSES - 1),
+                    )
+                if a == ROWS - 1:
+                    nc.vector.tensor_tensor(
+                        out=flat_grouped[:, cols, u, :],
+                        in0=sums[:].rearrange("p a n -> p n a"),
+                        in1=bias_all[:, e, cols].unsqueeze(2).to_broadcast([P, N_HALF, ROWS]),
+                        op=mybir.AluOpType.add,
+                    )
+            if u == 1 and a == ROWS - 1:
                 nc.vector.quantize_mx(
                     out=flat_codes[:, g2, :].bitcast(FP8X4),
                     scales=flat_planes[:, g2, :],
                     in_=flat_grouped[:].rearrange("p n u a -> p (n u a)"),
                 )
 
-        def combine_matmuls(c):
-            codes, planes = quantised[EXPERTS + c]
-            result = out_pool.tile([P, ROWS, D_OUT], F32)
-            for a in range(ROWS):
-                sums = sums_psum.tile([P, D_OUT], F32, tag="sums")
-                for g in range(PASSES):
-                    nc.tensor.matmul_mx(
-                        out=sums[:],
-                        lhsT=codes[:, g, a, :].bitcast(FP8X4),
-                        lhsT_scale=planes[:, g, a, :],
-                        rhs=flat_codes[:, g, :].bitcast(FP8X4),
-                        rhs_scale=flat_planes[:, g, :],
-                        start=(g == 0),
-                        stop=(g == PASSES - 1),
-                    )
-                nc.vector.tensor_copy(out=result[:, a, :], in_=sums[:])
-            nc.sync.dma_start(out=out_view[:, ROWS * c : ROWS * (c + 1), :], in_=result[:])
+        def combine_matmuls(c, a):
+            codes, planes = quantised[EXPERTS + c, a]
+            if a == 0:
+                result = out_pool.tile([P, ROWS, D_OUT], F32)
+                result_tiles[c] = result
+            result = result_tiles[c]
+            sums = sums_psum.tile([P, D_OUT], F32, tag="sums")
+            for g in range(PASSES):
+                nc.tensor.matmul_mx(
+                    out=sums[:],
+                    lhsT=codes[:, g, :].bitcast(FP8X4),
+                    lhsT_scale=planes[:, g, :],
+                    rhs=flat_codes[:, g, :].bitcast(FP8X4),
+                    rhs_scale=flat_planes[:, g, :],
+                    start=(g == 0),
+                    stop=(g == PASSES - 1),
+                )
+            nc.vector.tensor_copy(out=result[:, a, :], in_=sums[:])
+            if a == ROWS - 1:
+                nc.sync.dma_start(out=out_view[:, ROWS * c : ROWS * (c + 1), :], in_=result[:])
 
-        prepare(0)
-        for b in range(BLOCKS):
-            if b + 1 < BLOCKS:
-                prepare(b + 1)
+        def multiply(b, a):
             if b < EXPERTS:
-                expert_matmuls(b)
+                expert_matmuls(b, a)
             else:
-                combine_matmuls(b - EXPERTS)
+                combine_matmuls(b - EXPERTS, a)
+
+        units = ROWS * BLOCKS
+        x_units = ROWS * EXPERTS
+        prepare(*divmod(0, ROWS))
+        prepare(*divmod(1, ROWS))
+        for h in range(x_units - 2):
+            prepare(*divmod(h + 2, ROWS))
+            multiply(*divmod(h, ROWS))
+        for h in range(x_units - 2, units, 2):
+            for ahead in (h + 2, h + 3):
+                if ahead < units:
+                    prepare(*divmod(ahead, ROWS))
+            multiply(*divmod(h, ROWS))
+            multiply(*divmod(h + 1, ROWS))

@@ -218,13 +218,9 @@ def tile_expertparallelbehindblock_e_kernel(
                 combine_matmuls(b - EXPERTS, a)
 
         units = ROWS * BLOCKS
-        x_units = ROWS * EXPERTS
         prepare(*divmod(0, ROWS))
         prepare(*divmod(1, ROWS))
-        for h in range(x_units - 2):
-            prepare(*divmod(h + 2, ROWS))
-            multiply(*divmod(h, ROWS))
-        for h in range(x_units - 2, units, 2):
+        for h in range(0, units, 2):
             for ahead in (h + 2, h + 3):
                 if ahead < units:
                     prepare(*divmod(ahead, ROWS))

@@ -57,7 +57,7 @@ def tile_expertparallelbehindblock_e_kernel(
         grouped_pool = ctx.enter_context(tc.tile_pool(name="grouped", bufs=4))
         codes_pool = ctx.enter_context(tc.tile_pool(name="codes", bufs=4))
         flat_pool = ctx.enter_context(tc.tile_pool(name="flat", bufs=2))
-        out_pool = ctx.enter_context(tc.tile_pool(name="result", bufs=2))
+        out_pool = ctx.enter_context(tc.tile_pool(name="result", bufs=6))
         turned_psum = ctx.enter_context(tc.psum_pool(name="turned", bufs=4))
         sums_psum = ctx.enter_context(tc.psum_pool(name="sums", bufs=4))
         ctx.enter_context(tc.manual_schedule())
@@ -67,7 +67,6 @@ def tile_expertparallelbehindblock_e_kernel(
         quantised = {}
         flat_tiles = {}
         sums_tiles = {}
-        result_tiles = {}
 
         w_planes = const.tile([P, EXPERTS, D_OUT], U8, align_bytes=64)
         nc.vector.memset(w_planes[:].rearrange("p e n -> p (e n)").bitcast(I32), 0)
@@ -192,24 +191,28 @@ def tile_expertparallelbehindblock_e_kernel(
 
         def combine_matmuls(c, a):
             codes, planes = quantised[EXPERTS + c, a]
-            if a == 0:
-                result = out_pool.tile([P, ROWS, D_OUT], F32)
-                result_tiles[c] = result
-            result = result_tiles[c]
-            sums = sums_psum.tile([P, D_OUT], F32, tag="sums")
-            for g in range(PASSES):
-                nc.tensor.matmul_mx(
-                    out=sums[:],
-                    lhsT=codes[:, g, :].bitcast(FP8X4),
-                    lhsT_scale=planes[:, g, :],
-                    rhs=flat_codes[:, g, :].bitcast(FP8X4),
-                    rhs_scale=flat_planes[:, g, :],
-                    start=(g == 0),
-                    stop=(g == PASSES - 1),
-                )
-            nc.vector.tensor_copy(out=result[:, a, :], in_=sums[:])
-            if a == ROWS - 1:
-                nc.sync.dma_start(out=out_view[:, ROWS * c : ROWS * (c + 1), :], in_=result[:])
+            token_tile = ROWS * c + a
+            last_tile = token_tile == TOKEN_TILES - 1
+            width = N_HALF if last_tile else D_OUT
+            for first_col in range(0, D_OUT, width):
+                cols = slice(first_col, first_col + width)
+                sums = sums_psum.tile([P, width], F32, tag="sums")
+                for g in range(PASSES):
+                    nc.tensor.matmul_mx(
+                        out=sums[:],
+                        lhsT=codes[:, g, :].bitcast(FP8X4),
+                        lhsT_scale=planes[:, g, :],
+                        rhs=flat_codes[:, g, cols].bitcast(FP8X4),
+                        rhs_scale=flat_planes[:, g, cols],
+                        start=(g == 0),
+                        stop=(g == PASSES - 1),
+                    )
+                result = out_pool.tile([P, width], F32, tag="result")
+                if last_tile and first_col > 0:
+                    nc.scalar.copy(out=result[:], in_=sums[:])
+                else:
+                    nc.vector.tensor_copy(out=result[:], in_=sums[:])
+                nc.sync.dma_start(out=out_view[:, token_tile, cols], in_=result[:])
 
         def multiply(b, a):
             if b < EXPERTS:

from contextlib import ExitStack

import concourse.mybir as mybir
from concourse.masks import make_identity

F32 = mybir.dt.float32
BF16 = mybir.dt.bfloat16
I32 = mybir.dt.int32
U32 = mybir.dt.uint32
U8 = mybir.dt.uint8
FP8X4 = mybir.dt.float8_e4m3fn_x4

P = 128
PACK = 4
K_PASS = P * PACK
K_WORDS = K_PASS // 2

EXPERTS = 8
CAP = 256
D_IN = 2048
D_OUT = 512
TOKENS = 1024
ROW_LEN = 2048
PASSES = ROW_LEN // K_PASS
ROWS = 2
TOKEN_TILES = TOKENS // P
CW_BLOCKS = TOKEN_TILES // ROWS
BLOCKS = EXPERTS + CW_BLOCKS
N_HALF = D_OUT // 2

FLOPS = 2 * EXPERTS * CAP * D_IN * D_OUT + 2 * TOKENS * EXPERTS * CAP * D_OUT


def every_second_word(g, u):
    return slice(K_WORDS * g + u, K_WORDS * (g + 1), 2)


def half_of_the_words(g, u):
    return slice(K_WORDS * g + P * u, K_WORDS * g + P * (u + 1))


def tile_expertparallelbehindblock_e_kernel(
    tc, inputs, combine_weights, weight_words, weight_scales, bias, out
):
    nc = tc.nc

    x_view = inputs.rearrange("(e p a) k -> e p a k", p=P, a=ROWS)
    cw_view = combine_weights.rearrange("(p t) e c -> p t (e c)", t=TOKEN_TILES)
    out_view = out.rearrange("b l n -> (b l) n").rearrange("(p t) n -> p t n", t=TOKEN_TILES)
    words_view = weight_words.rearrange("(e g) p n t -> e p g (n t)", g=PASSES)
    scales_view = weight_scales.rearrange("(e g) (q r) n -> e q g r n", g=PASSES, r=4)

    with ExitStack() as ctx:
        const = ctx.enter_context(tc.tile_pool(name="const", bufs=1))
        raw_pool = ctx.enter_context(tc.tile_pool(name="raw", bufs=BLOCKS))
        words_pool = ctx.enter_context(tc.tile_pool(name="words", bufs=EXPERTS))
        grouped_pool = ctx.enter_context(tc.tile_pool(name="grouped", bufs=4))
        codes_pool = ctx.enter_context(tc.tile_pool(name="codes", bufs=4))
        flat_pool = ctx.enter_context(tc.tile_pool(name="flat", bufs=2))
        out_pool = ctx.enter_context(tc.tile_pool(name="result", bufs=6))
        turned_psum = ctx.enter_context(tc.psum_pool(name="turned", bufs=4))
        sums_psum = ctx.enter_context(tc.psum_pool(name="sums", bufs=4))
        ctx.enter_context(tc.manual_schedule())

        raw_tiles = {}
        word_tiles = {}
        quantised = {}
        flat_tiles = {}
        sums_tiles = {}

        w_planes = const.tile([P, EXPERTS, D_OUT], U8, align_bytes=64)
        nc.vector.memset(w_planes[:].rearrange("p e n -> p (e n)").bitcast(I32), 0)
        flat_codes = const.tile([P, PASSES, D_OUT], U32, align_bytes=64)
        flat_planes = const.tile([P, PASSES, D_OUT], U8, align_bytes=64)

        def load_raw(b):
            raw = raw_pool.tile([P, ROWS, ROW_LEN], BF16)
            if b < EXPERTS:
                nc.sync.dma_start(out=raw[:], in_=x_view[b])
            else:
                first = ROWS * (b - EXPERTS)
                nc.sync.dma_start(out=raw[:], in_=cw_view[:, first : first + ROWS, :])
            raw_tiles[b] = raw

        def load_for_block(b):
            if b < EXPERTS:
                for q in range(4):
                    nc.sync.dma_start(
                        out=w_planes[32 * q : 32 * q + 16, b, :].bitcast(I32),
                        in_=scales_view[b, q].bitcast(I32),
                    )
            if b + 1 < BLOCKS:
                load_raw(b + 1)
            if b < EXPERTS:
                w_words = words_pool.tile([P, PASSES, D_OUT], U32, align_bytes=64)
                nc.sync.dma_start(out=w_words[:].bitcast(I32), in_=words_view[b].bitcast(I32))
                word_tiles[b] = w_words

        bias_rows = const.tile([P, D_OUT], BF16)
        nc.sync.dma_start(
            out=bias_rows[:],
            in_=bias.rearrange("e o n -> o e n").to_broadcast([P // EXPERTS, EXPERTS, D_OUT]),
        )

        load_raw(0)
        for b in range(BLOCKS):
            load_for_block(b)

        ident_bf = const.tile([P, P], BF16)
        make_identity(nc, ident_bf[:])
        ident_f32 = const.tile([P, P], F32)
        make_identity(nc, ident_f32[:])
        bias_all = const.tile([P, EXPERTS, D_OUT], BF16)
        for e in range(EXPERTS):
            spread = sums_psum.tile([P, D_OUT], F32, tag="sums")
            nc.tensor.matmul(
                out=spread[:],
                lhsT=ident_bf[:, e : e + 1].to_broadcast([P, P]),
                rhs=bias_rows[:],
                start=True,
                stop=True,
            )
            if e % 2 == 0:
                nc.vector.tensor_copy(out=bias_all[:, e, :], in_=spread[:])
            else:
                nc.scalar.copy(out=bias_all[:, e, :], in_=spread[:])

        def prepare(b, a):
            raw_words = raw_tiles[b][:, a, :].bitcast(F32)
            word_columns = every_second_word if b < EXPERTS else half_of_the_words
            grouped = grouped_pool.tile([P, PASSES, P, PACK], BF16, align_bytes=64)
            for first_pass in range(0, PASSES, 2):
                turned = turned_psum.tile([P, 2, 2, P], F32, tag="turned")
                for i in range(2):
                    for u in range(2):
                        nc.tensor.transpose(
                            turned[:, i, u, :],
                            raw_words[:, word_columns(first_pass + i, u)],
                            ident_f32[:],
                        )
                nc.scalar.copy(
                    out=grouped[:, first_pass : first_pass + 2].bitcast(F32),
                    in_=turned[:].rearrange("p i u r -> p i r u"),
                )
            codes = codes_pool.tile([P, PASSES, P], U32, align_bytes=64)
            planes = codes_pool.tile([P, PASSES, P], U8, align_bytes=64)
            nc.vector.quantize_mx(
                out=codes[:].rearrange("p g r -> p (g r)").bitcast(FP8X4),
                scales=planes[:].rearrange("p g r -> p (g r)"),
                in_=grouped[:].rearrange("p g r t -> p (g r t)"),
            )
            quantised[b, a] = (codes, planes)

        def expert_matmuls(e, a):
            codes, planes = quantised[e, a]
            w_words = word_tiles[e]
            g2, u = divmod(e, 2)
            if u == 0 and a == 0:
                flat_grouped = flat_pool.tile([P, D_OUT, 2, ROWS], BF16, align_bytes=64)
                flat_tiles[g2] = flat_grouped
            flat_grouped = flat_tiles[g2]
            for half in range(D_OUT // N_HALF):
                cols = slice(half * N_HALF, (half + 1) * N_HALF)
                if a == 0:
                    sums = sums_psum.tile([P, ROWS, N_HALF], F32, tag="sums")
                    sums_tiles[e, half] = sums
                sums = sums_tiles[e, half]
                for g in range(PASSES):
                    nc.tensor.matmul_mx(
                        out=sums[:, a, :],
                        lhsT=codes[:, g, :].bitcast(FP8X4),
                        lhsT_scale=planes[:, g, :],
                        rhs=w_words[:, g, cols].bitcast(FP8X4),
                        rhs_scale=w_planes[4 * g : P, e, cols],
                        start=(g == 0),
                        stop=(g == PASSES - 1),
                    )
                if a == ROWS - 1:
                    nc.vector.tensor_tensor(
                        out=flat_grouped[:, cols, u, :],
                        in0=sums[:].rearrange("p a n -> p n a"),
                        in1=bias_all[:, e, cols].unsqueeze(2).to_broadcast([P, N_HALF, ROWS]),
                        op=mybir.AluOpType.add,
                    )
            if u == 1 and a == ROWS - 1:
                nc.vector.quantize_mx(
                    out=flat_codes[:, g2, :].bitcast(FP8X4),
                    scales=flat_planes[:, g2, :],
                    in_=flat_grouped[:].rearrange("p n u a -> p (n u a)"),
                )

        def combine_matmuls(c, a):
            codes, planes = quantised[EXPERTS + c, a]
            token_tile = ROWS * c + a
            last_tile = token_tile == TOKEN_TILES - 1
            width = N_HALF if last_tile else D_OUT
            for first_col in range(0, D_OUT, width):
                cols = slice(first_col, first_col + width)
                sums = sums_psum.tile([P, width], F32, tag="sums")
                for g in range(PASSES):
                    nc.tensor.matmul_mx(
                        out=sums[:],
                        lhsT=codes[:, g, :].bitcast(FP8X4),
                        lhsT_scale=planes[:, g, :],
                        rhs=flat_codes[:, g, cols].bitcast(FP8X4),
                        rhs_scale=flat_planes[:, g, cols],
                        start=(g == 0),
                        stop=(g == PASSES - 1),
                    )
                result = out_pool.tile([P, width], F32, tag="result")
                if last_tile and first_col > 0:
                    nc.scalar.copy(out=result[:], in_=sums[:])
                else:
                    nc.vector.tensor_copy(out=result[:], in_=sums[:])
                nc.sync.dma_start(out=out_view[:, token_tile, cols], in_=result[:])

        def multiply(b, a):
            if b < EXPERTS:
                expert_matmuls(b, a)
            else:
                combine_matmuls(b - EXPERTS, a)

        units = ROWS * BLOCKS
        prepare(*divmod(0, ROWS))
        prepare(*divmod(1, ROWS))
        for h in range(0, units, 2):
            for ahead in (h + 2, h + 3):
                if ahead < units:
                    prepare(*divmod(ahead, ROWS))
            multiply(*divmod(h, ROWS))
            multiply(*divmod(h + 1, ROWS))
